import numpy as np
import ml_dtypes


def mxq(x, axis, fmt="e4m3"):
    dtype, down = {"e4m3": (ml_dtypes.float8_e4m3fn, 7), "e5m2": (ml_dtypes.float8_e5m2, 14)}[fmt]
    v = np.moveaxis(np.asarray(x, np.float32).astype(ml_dtypes.bfloat16).astype(np.float64), axis, -1)
    blocks = v.reshape(v.shape[:-1] + (-1, 32))
    amax = np.abs(blocks).max(-1, keepdims=True)
    byte = np.maximum(np.where(amax > 0, np.frexp(amax)[1] - 1 + 127, 0) - down, 1)
    scale = np.exp2(byte - 127.0)
    codes = (blocks / scale).astype(np.float32).astype(dtype).astype(np.float64)
    return np.moveaxis((codes * scale).reshape(v.shape), -1, axis)


WIDE = False


def mx_kscale(k):
    if not WIDE:
        return np.ones(k)
    levels = np.array([10, -10, 5, -5, 0])
    a = np.random.permutation(np.resize(levels, k // 512 * 4)).reshape(k // 512, 4)
    idx = np.arange(k)
    return np.exp2(a[idx // 512, idx % 128 // 32])


BF16 = ml_dtypes.bfloat16


def bf(x):
    return np.asarray(x, np.float32).astype(BF16)


def f64(x):
    return np.asarray(x).astype(np.float64)


E2M1 = np.array([0.0, 0.5, 1.0, 1.5, 2.0, 3.0, 4.0, 6.0, -0.0, -0.5, -1.0, -1.5, -2.0, -3.0, -4.0, -6.0])


def pack_weight(w, fmt):
    k, n = w.shape
    w = f64(bf(w)).reshape(k // 32, 32, n)
    amax = np.abs(w).max(1)
    if fmt == "e4m3":
        byte = np.frexp(amax)[1] - 1 + 127 - 7
    else:
        mant, ex = np.frexp(amax / 6.0)
        byte = np.where(mant > 0.5, ex, ex - 1) + 127
    byte = np.clip(np.where(amax > 0, byte, 1), 1, 254)
    scaled = (w * np.exp2(127.0 - byte)[:, None, :]).reshape(k, n).astype(np.float32)
    by_word = np.ascontiguousarray(scaled.reshape(k // 512, 128, 4, n).transpose(0, 1, 3, 2))
    if fmt == "e4m3":
        words = by_word.astype(ml_dtypes.float8_e4m3fn).view(np.uint8)
    else:
        c = by_word.astype(ml_dtypes.float4_e2m1fn).view(np.uint8) & 0xF
        words = c[..., 0::2] | (c[..., 1::2] << 4)
    return np.ascontiguousarray(words), np.ascontiguousarray(byte.astype(np.uint8).reshape(k // 512, 16, n))


def unpack_weight(words, scales, fmt):
    g, p, n, _ = words.shape
    if fmt == "e4m3":
        vals = np.ascontiguousarray(words).view(ml_dtypes.float8_e4m3fn).astype(np.float64)
    else:
        nib = np.empty((g, p, n, 4), np.uint8)
        nib[..., 0::2] = words & 0xF
        nib[..., 1::2] = words >> 4
        vals = E2M1[nib]
    vals = vals * np.repeat(np.exp2(scales.astype(np.float64) - 127.0), 8, axis=1)[..., None]
    return vals.transpose(0, 1, 3, 2).reshape(g * 512, n)


B, MI, MO, NL = 384, 512, 1024, 4
IR_DIMS = tuple(2 * l + 1 for l in range(NL))
FLAT_IN = MI * sum(IR_DIMS)
FMT = "e4m3"


def setup_inputs():
    s = mx_kscale(MI)
    sx = np.concatenate([np.repeat(s, d) for d in IR_DIMS])
    inp = {"x": bf(np.random.standard_normal((B, FLAT_IN)) * sx)}
    for l in range(NL):
        w = np.random.standard_normal((MO, MI)) / np.sqrt(MI) / s[None, :]
        words, scales = pack_weight(w.T, FMT)
        inp["W%d_words" % l] = words
        inp["W%d_scales" % l] = scales
    inp["bias"] = bf(np.random.standard_normal(MO))
    return inp


def reference(x, W0_words, W0_scales, W1_words, W1_scales, W2_words, W2_scales, W3_words, W3_scales, bias):
    x = f64(x)
    outs = []
    start = 0
    packed = ((W0_words, W0_scales), (W1_words, W1_scales), (W2_words, W2_scales), (W3_words, W3_scales))
    for d, (words, scales) in zip(IR_DIMS, packed):
        seg = x[:, start:start + MI * d].reshape(B, MI, d)
        rows = seg.transpose(0, 2, 1).reshape(B * d, MI)
        y = mxq(rows, 1, "e4m3") @ unpack_weight(words, scales, FMT)
        outs.append(y.reshape(B, d, MO).transpose(0, 2, 1).reshape(B, MO * d))
        start += MI * d
    outs[0] = outs[0] + f64(bias)
    return np.concatenate(outs, axis=1)

@@ -1,0 +1,197 @@
+from contextlib import ExitStack
+
+import concourse.mybir as mybir
+from concourse.masks import make_identity
+
+BF16 = mybir.dt.bfloat16
+F32 = mybir.dt.float32
+I32 = mybir.dt.int32
+U32 = mybir.dt.uint32
+U8 = mybir.dt.uint8
+FP8X4 = mybir.dt.float8_e4m3fn_x4
+
+P = 128
+BATCH = 384
+CH_IN = 512
+CH_OUT = 1024
+IR_DIMS = (1, 3, 5, 7)
+BANK = 512
+BATCH_TILES = BATCH // P
+
+FLOPS = 2 * BATCH * sum(IR_DIMS) * CH_IN * CH_OUT
+
+KEPT = (512, 128, 64, 64)
+WIDTH = (512, 128, 128, 128)
+SPILL = 64
+
+BANKS_PER_STORE = 4
+SORT_RUNS = 4
+LOOKAHEAD = 2
+
+
+def tile_so3_linear_pa_t_kernel(
+    tc, x, W0_words, W0_scales, W1_words, W1_scales, W2_words, W2_scales, W3_words, W3_scales, bias, out
+):
+    nc = tc.nc
+    w_words_in = (W0_words, W1_words, W2_words, W3_words)
+    w_scales_in = (W0_scales, W1_scales, W2_scales, W3_scales)
+    x_start = [CH_IN * sum(IR_DIMS[:l]) for l in range(4)]
+    out_start = [CH_OUT * sum(IR_DIMS[:l]) for l in range(4)]
+    units = [(bt, l) for bt in range(BATCH_TILES) for l in range(4)]
+
+    with ExitStack() as ctx:
+        const = ctx.enter_context(tc.tile_pool(name="const", bufs=1))
+        x_pool = ctx.enter_context(tc.tile_pool(name="x_pool", bufs=BATCH_TILES))
+        sort_pool = ctx.enter_context(tc.tile_pool(name="sort_pool", bufs=3))
+        group_pool = ctx.enter_context(tc.tile_pool(name="group_pool", bufs=2))
+        code_pool = ctx.enter_context(tc.tile_pool(name="code_pool", bufs=LOOKAHEAD + 2))
+        stage_pool = ctx.enter_context(tc.tile_pool(name="stage_pool", bufs=6))
+        xt_pool = ctx.enter_context(tc.psum_pool(name="xt_pool", bufs=4))
+        acc_pool = ctx.enter_context(tc.psum_pool(name="acc_pool", bufs=4))
+
+        w_planes = const.tile([P, CH_OUT + SPILL], U8, align_bytes=64)
+        nc.vector.memset(w_planes[:].bitcast(I32), 0)
+        w_words = const.tile([P, 4 * CH_OUT + SPILL], U32, align_bytes=64)
+        nc.vector.memset(w_words[:, 4 * CH_OUT :].bitcast(I32), 0)
+        bias_rows = const.tile([P, CH_OUT], BF16)
+        nc.vector.memset(bias_rows[:], 0.0)
+        ones = const.tile([P, P], BF16)
+        nc.vector.memset(ones[:], 1.0)
+        ident = const.tile([P, P], F32)
+        make_identity(nc, ident[:])
+        nc.scalar.dma_start(out=bias_rows[0:1, :], in_=bias.unsqueeze(0))
+
+        x_tiles = {}
+
+        def load_x(bt, l):
+            x_seg = x_pool.tile([P, CH_IN * IR_DIMS[l]], BF16, tag="x%d" % l)
+            nc.sync.dma_start(
+                out=x_seg[:],
+                in_=x[bt * P : (bt + 1) * P, x_start[l] : x_start[l] + CH_IN * IR_DIMS[l]],
+            )
+            x_tiles[(bt, l)] = x_seg
+
+        def load_w_words(l):
+            nc.sync.dma_start(
+                out=w_words[:, l * CH_OUT : (l + 1) * CH_OUT].bitcast(I32),
+                in_=w_words_in[l].rearrange("g p n t -> (g p) (n t)").bitcast(I32),
+            )
+
+        load_x(0, 0)
+        load_x(0, 1)
+        for l in range(4):
+            rows = w_scales_in[l].rearrange("g (q r) n -> r (g q) n", r=4)
+            for r in range(4):
+                nc.sync.dma_start(
+                    out=w_planes[4 * l + r : P : 32, 0:CH_OUT].bitcast(I32), in_=rows[r].bitcast(I32)
+                )
+        load_w_words(0)
+        load_w_words(1)
+        load_x(0, 2)
+        load_w_words(2)
+        load_x(0, 3)
+        load_w_words(3)
+        for bt in range(1, BATCH_TILES):
+            for l in range(4):
+                load_x(bt, l)
+
+        bias_f32 = const.tile([P, CH_OUT], F32)
+        for h in range(CH_OUT // BANK):
+            cols = slice(h * BANK, (h + 1) * BANK)
+            bias_acc = acc_pool.tile([P, BANK], F32, tag="acc")
+            nc.tensor.matmul(out=bias_acc[:], lhsT=ones[:], rhs=bias_rows[:, cols], start=True, stop=True)
+            nc.vector.tensor_copy(out=bias_f32[:, cols], in_=bias_acc[:])
+
+        sorted_tiles = {}
+        code_tiles = {}
+
+        def sort_unit(bt, l):
+            d = IR_DIMS[l]
+            x_seg = x_tiles[(bt, l)]
+            xs = sort_pool.tile([P, CH_IN * d], BF16, tag="xs")
+            src = x_seg[:].rearrange("b (p u e i) -> b u p e i", u=2, e=2, i=d)
+            dst = xs[:].rearrange("b (i u p e) -> b u p e i", u=2, p=P, e=2)
+            for i0 in range(0, d, SORT_RUNS):
+                i1 = min(i0 + SORT_RUNS, d)
+                for u in range(2):
+                    nc.vector.tensor_copy(out=dst[:, u, :, :, i0:i1], in_=src[:, u, :, :, i0:i1])
+            sorted_tiles[(bt, l)] = xs
+
+        def quantise_unit(bt, l):
+            d = IR_DIMS[l]
+            xs_words = sorted_tiles[(bt, l)][:].bitcast(F32)
+            grouped = group_pool.tile([P, CH_IN * d], BF16, tag="grouped", align_bytes=64)
+            grouped_words = grouped[:].bitcast(F32)
+            codes = code_pool.tile([P, P * d], U32, tag="codes", align_bytes=64)
+            plane = code_pool.tile([P, P * d], U8, tag="plane", align_bytes=64)
+            pairs = [(i0, min(i0 + 2, d)) for i0 in range(0, d, 2)]
+            banks = []
+            for i0, i1 in pairs:
+                xt = xt_pool.tile([P, 4, P], F32, tag="xt")
+                for s in range(2 * (i1 - i0)):
+                    w0 = (2 * i0 + s) * P
+                    nc.tensor.transpose(out=xt[:, s, :], in_=xs_words[:, w0 : w0 + P], identity=ident[:])
+                banks.append(xt)
+            for (i0, i1), xt in zip(pairs, banks):
+                nc.scalar.copy(
+                    out=grouped_words[:, i0 * 2 * P : i1 * 2 * P].rearrange("p (i b u) -> p i b u", i=i1 - i0, u=2),
+                    in_=xt[:, 0 : 2 * (i1 - i0), :].rearrange("p (i u) b -> p i b u", u=2),
+                )
+            for i0, i1 in pairs:
+                nc.vector.quantize_mx(
+                    out=codes[:, i0 * P : i1 * P].bitcast(FP8X4),
+                    scales=plane[:, i0 * P : i1 * P],
+                    in_=grouped[:, i0 * 4 * P : i1 * 4 * P],
+                )
+            code_tiles[(bt, l)] = (codes, plane)
+
+        def multiply_unit(bt, l):
+            d = IR_DIMS[l]
+            kept = KEPT[l]
+            width = WIDTH[l]
+            codes, plane = code_tiles[(bt, l)]
+            n_banks = CH_OUT // kept
+            per_store = min(BANKS_PER_STORE, n_banks)
+            for first in range(0, n_banks, per_store):
+                stage = stage_pool.tile([P, per_store * d * kept], F32, tag="stage")
+                for k in range(per_store):
+                    n0 = (first + k) * kept
+                    acc = acc_pool.tile([P, BANK], F32, tag="acc")
+                    for i in range(d):
+                        nc.tensor.matmul_mx(
+                            out=acc[:, i * kept : i * kept + width],
+                            lhsT=codes[:, i * P : (i + 1) * P].bitcast(FP8X4),
+                            lhsT_scale=plane[:, i * P : (i + 1) * P],
+                            rhs=w_words[:, l * CH_OUT + n0 : l * CH_OUT + n0 + width].bitcast(FP8X4),
+                            rhs_scale=w_planes[4 * l : P, n0 : n0 + width],
+                            start=True,
+                            stop=True,
+                        )
+                    dst = stage[:, k * d * kept : (k + 1) * d * kept]
+                    if l == 0:
+                        nc.vector.tensor_tensor(
+                            out=dst, in0=acc[:], in1=bias_f32[:, n0 : n0 + kept], op=mybir.AluOpType.add
+                        )
+                    else:
+                        dst = dst.rearrange("p (n i) -> p n i", i=d)
+                        src = acc[:, 0 : d * kept].rearrange("p (i n) -> p n i", i=d)
+                        if (first + k) % 3 == 2:
+                            nc.vector.tensor_copy(out=dst, in_=src)
+                        else:
+                            nc.scalar.copy(out=dst, in_=src)
+                c0 = out_start[l] + first * d * kept
+                nc.sync.dma_start(
+                    out=out[bt * P : (bt + 1) * P, c0 : c0 + per_store * d * kept], in_=stage[:]
+                )
+
+        n_units = len(units)
+        for j in range(LOOKAHEAD + 1):
+            sort_unit(*units[j])
+        for j in range(LOOKAHEAD):
+            quantise_unit(*units[j])
+        for j in range(n_units):
+            if j + LOOKAHEAD + 1 < n_units:
+                sort_unit(*units[j + LOOKAHEAD + 1])
+            if j + LOOKAHEAD < n_units:
+                quantise_unit(*units[j + LOOKAHEAD])
+            multiply_unit(*units[j])

@@ -24,9 +24,12 @@ KEPT = (512, 128, 64, 64)
 WIDTH = (512, 128, 128, 128)
 SPILL = 64
 
+L_ORDER = (0, 1, 3, 2)
+BY_PLANES = 3
 BANKS_PER_STORE = 4
+STAGE_COLS = 1792
 SORT_RUNS = 4
-LOOKAHEAD = 2
+LOOKAHEAD = 3
 
 
 def tile_so3_linear_pa_t_kernel(
@@ -37,15 +40,16 @@ def tile_so3_linear_pa_t_kernel(
     w_scales_in = (W0_scales, W1_scales, W2_scales, W3_scales)
     x_start = [CH_IN * sum(IR_DIMS[:l]) for l in range(4)]
     out_start = [CH_OUT * sum(IR_DIMS[:l]) for l in range(4)]
-    units = [(bt, l) for bt in range(BATCH_TILES) for l in range(4)]
+    units = [(bt, l) for bt in range(BATCH_TILES) for l in L_ORDER]
 
     with ExitStack() as ctx:
         const = ctx.enter_context(tc.tile_pool(name="const", bufs=1))
-        x_pool = ctx.enter_context(tc.tile_pool(name="x_pool", bufs=BATCH_TILES))
+        x_pool = ctx.enter_context(tc.tile_pool(name="x_pool", bufs=2))
         sort_pool = ctx.enter_context(tc.tile_pool(name="sort_pool", bufs=3))
         group_pool = ctx.enter_context(tc.tile_pool(name="group_pool", bufs=2))
         code_pool = ctx.enter_context(tc.tile_pool(name="code_pool", bufs=LOOKAHEAD + 2))
-        stage_pool = ctx.enter_context(tc.tile_pool(name="stage_pool", bufs=6))
+        stage_pool = ctx.enter_context(tc.tile_pool(name="stage_pool", bufs=12))
+        plane_pool = ctx.enter_context(tc.tile_pool(name="plane_pool", bufs=2))
         xt_pool = ctx.enter_context(tc.psum_pool(name="xt_pool", bufs=4))
         acc_pool = ctx.enter_context(tc.psum_pool(name="acc_pool", bufs=4))
 
@@ -87,12 +91,12 @@ def tile_so3_linear_pa_t_kernel(
                 )
         load_w_words(0)
         load_w_words(1)
-        load_x(0, 2)
-        load_w_words(2)
         load_x(0, 3)
         load_w_words(3)
+        load_x(0, 2)
+        load_w_words(2)
         for bt in range(1, BATCH_TILES):
-            for l in range(4):
+            for l in L_ORDER:
                 load_x(bt, l)
 
         bias_f32 = const.tile([P, CH_OUT], F32)
@@ -184,6 +188,47 @@ def tile_so3_linear_pa_t_kernel(
                     out=out[bt * P : (bt + 1) * P, c0 : c0 + per_store * d * kept], in_=stage[:]
                 )
 
+        def multiply_by_planes(bt, l):
+            d = IR_DIMS[l]
+            codes, plane = code_tiles[(bt, l)]
+            n_stage = STAGE_COLS // d
+            for h in range(CH_OUT // BANK):
+                n0 = h * BANK
+                planes = plane_pool.tile([P, d, BANK], F32, tag="planes")
+                for i in range(d):
+                    acc = acc_pool.tile([P, BANK], F32, tag="acc")
+                    nc.tensor.matmul_mx(
+                        out=acc[:],
+                        lhsT=codes[:, i * P : (i + 1) * P].bitcast(FP8X4),
+                        lhsT_scale=plane[:, i * P : (i + 1) * P],
+                        rhs=w_words[:, l * CH_OUT + n0 : l * CH_OUT + n0 + BANK].bitcast(FP8X4),
+                        rhs_scale=w_planes[4 * l : P, n0 : n0 + BANK],
+                        start=True,
+                        stop=True,
+                    )
+                    if i % 2 == 0:
+                        nc.scalar.copy(out=planes[:, i, :], in_=acc[:])
+                    else:
+                        nc.vector.tensor_copy(out=planes[:, i, :], in_=acc[:])
+                for q in range(BANK // n_stage):
+                    stage = stage_pool.tile([P, STAGE_COLS], F32, tag="stage")
+                    nc.gpsimd.tensor_scalar(
+                        out=stage[:].rearrange("p (n i) -> p n i", i=d),
+                        in0=planes[:, :, q * n_stage : (q + 1) * n_stage].rearrange("p i n -> p n i"),
+                        scalar1=1.0,
+                        scalar2=0.0,
+                        op0=mybir.AluOpType.mult,
+                        op1=mybir.AluOpType.add,
+                    )
+                    c0 = out_start[l] + (n0 + q * n_stage) * d
+                    nc.sync.dma_start(out=out[bt * P : (bt + 1) * P, c0 : c0 + STAGE_COLS], in_=stage[:])
+
+        def multiply(bt, l):
+            if l == BY_PLANES:
+                multiply_by_planes(bt, l)
+            else:
+                multiply_unit(bt, l)
+
         n_units = len(units)
         for j in range(LOOKAHEAD + 1):
             sort_unit(*units[j])
@@ -194,4 +239,4 @@ def tile_so3_linear_pa_t_kernel(
                 sort_unit(*units[j + LOOKAHEAD + 1])
             if j + LOOKAHEAD < n_units:
                 quantise_unit(*units[j + LOOKAHEAD])
-            multiply_unit(*units[j])
+            multiply(*units[j])

@@ -20,16 +20,15 @@ BATCH_TILES = BATCH // P
 
 FLOPS = 2 * BATCH * sum(IR_DIMS) * CH_IN * CH_OUT
 
-KEPT = (512, 128, 64, 64)
 WIDTH = (512, 128, 128, 128)
+KEPT = (512, 128, 96, 64)
 SPILL = 64
+WINDOW = 64
+MOVED = 32
 
-L_ORDER = (0, 1, 3, 2)
-BY_PLANES = 3
 BANKS_PER_STORE = 4
-STAGE_COLS = 1792
 SORT_RUNS = 4
-LOOKAHEAD = 3
+LOOKAHEAD = 2
 
 
 def tile_so3_linear_pa_t_kernel(
@@ -40,16 +39,15 @@ def tile_so3_linear_pa_t_kernel(
     w_scales_in = (W0_scales, W1_scales, W2_scales, W3_scales)
     x_start = [CH_IN * sum(IR_DIMS[:l]) for l in range(4)]
     out_start = [CH_OUT * sum(IR_DIMS[:l]) for l in range(4)]
-    units = [(bt, l) for bt in range(BATCH_TILES) for l in L_ORDER]
+    units = [(bt, l) for bt in range(BATCH_TILES) for l in range(4)]
 
     with ExitStack() as ctx:
         const = ctx.enter_context(tc.tile_pool(name="const", bufs=1))
-        x_pool = ctx.enter_context(tc.tile_pool(name="x_pool", bufs=2))
+        x_pool = ctx.enter_context(tc.tile_pool(name="x_pool", bufs=BATCH_TILES))
         sort_pool = ctx.enter_context(tc.tile_pool(name="sort_pool", bufs=3))
         group_pool = ctx.enter_context(tc.tile_pool(name="group_pool", bufs=2))
         code_pool = ctx.enter_context(tc.tile_pool(name="code_pool", bufs=LOOKAHEAD + 2))
         stage_pool = ctx.enter_context(tc.tile_pool(name="stage_pool", bufs=12))
-        plane_pool = ctx.enter_context(tc.tile_pool(name="plane_pool", bufs=2))
         xt_pool = ctx.enter_context(tc.psum_pool(name="xt_pool", bufs=4))
         acc_pool = ctx.enter_context(tc.psum_pool(name="acc_pool", bufs=4))
 
@@ -91,13 +89,16 @@ def tile_so3_linear_pa_t_kernel(
                 )
         load_w_words(0)
         load_w_words(1)
-        load_x(0, 3)
-        load_w_words(3)
         load_x(0, 2)
         load_w_words(2)
+        load_x(0, 3)
+        load_w_words(3)
         for bt in range(1, BATCH_TILES):
-            for l in L_ORDER:
+            for l in range(4):
                 load_x(bt, l)
+
+        w_planes_moved = const.tile([P, MOVED + CH_OUT + SPILL], U8, align_bytes=64)
+        nc.vector.tensor_copy(out=w_planes_moved[:, MOVED:].bitcast(I32), in_=w_planes[:].bitcast(I32))
 
         bias_f32 = const.tile([P, CH_OUT], F32)
         for h in range(CH_OUT // BANK):
@@ -154,12 +155,17 @@ def tile_so3_linear_pa_t_kernel(
             kept = KEPT[l]
             width = WIDTH[l]
             codes, plane = code_tiles[(bt, l)]
-            n_banks = CH_OUT // kept
-            per_store = min(BANKS_PER_STORE, n_banks)
-            for first in range(0, n_banks, per_store):
-                stage = stage_pool.tile([P, per_store * d * kept], F32, tag="stage")
-                for k in range(per_store):
-                    n0 = (first + k) * kept
+            ranges = [(n0, min(kept, CH_OUT - n0)) for n0 in range(0, CH_OUT, kept)]
+            for first in range(0, len(ranges), BANKS_PER_STORE):
+                group = ranges[first : first + BANKS_PER_STORE]
+                n_first = group[0][0]
+                n_group = sum(n_here for n0, n_here in group)
+                stage = stage_pool.tile([P, n_group * d], F32, tag="stage")
+                for k, (n0, n_here) in enumerate(group):
+                    if n0 % WINDOW == 0:
+                        rhs_scale = w_planes[4 * l : P, n0 : n0 + width]
+                    else:
+                        rhs_scale = w_planes_moved[4 * l : P, MOVED + n0 : MOVED + n0 + width]
                     acc = acc_pool.tile([P, BANK], F32, tag="acc")
                     for i in range(d):
                         nc.tensor.matmul_mx(
@@ -167,67 +173,24 @@ def tile_so3_linear_pa_t_kernel(
                             lhsT=codes[:, i * P : (i + 1) * P].bitcast(FP8X4),
                             lhsT_scale=plane[:, i * P : (i + 1) * P],
                             rhs=w_words[:, l * CH_OUT + n0 : l * CH_OUT + n0 + width].bitcast(FP8X4),
-                            rhs_scale=w_planes[4 * l : P, n0 : n0 + width],
+                            rhs_scale=rhs_scale,
                             start=True,
                             stop=True,
                         )
-                    dst = stage[:, k * d * kept : (k + 1) * d * kept]
+                    dst = stage[:, (n0 - n_first) * d : (n0 - n_first + n_here) * d]
                     if l == 0:
                         nc.vector.tensor_tensor(
-                            out=dst, in0=acc[:], in1=bias_f32[:, n0 : n0 + kept], op=mybir.AluOpType.add
+                            out=dst, in0=acc[:], in1=bias_f32[:, n0 : n0 + n_here], op=mybir.AluOpType.add
                         )
                     else:
                         dst = dst.rearrange("p (n i) -> p n i", i=d)
-                        src = acc[:, 0 : d * kept].rearrange("p (i n) -> p n i", i=d)
+                        src = acc[:, 0 : d * kept].rearrange("p (i n) -> p n i", i=d)[:, 0:n_here, :]
                         if (first + k) % 3 == 2:
                             nc.vector.tensor_copy(out=dst, in_=src)
                         else:
                             nc.scalar.copy(out=dst, in_=src)
-                c0 = out_start[l] + first * d * kept
-                nc.sync.dma_start(
-                    out=out[bt * P : (bt + 1) * P, c0 : c0 + per_store * d * kept], in_=stage[:]
-                )
-
-        def multiply_by_planes(bt, l):
-            d = IR_DIMS[l]
-            codes, plane = code_tiles[(bt, l)]
-            n_stage = STAGE_COLS // d
-            for h in range(CH_OUT // BANK):
-                n0 = h * BANK
-                planes = plane_pool.tile([P, d, BANK], F32, tag="planes")
-                for i in range(d):
-                    acc = acc_pool.tile([P, BANK], F32, tag="acc")
-                    nc.tensor.matmul_mx(
-                        out=acc[:],
-                        lhsT=codes[:, i * P : (i + 1) * P].bitcast(FP8X4),
-                        lhsT_scale=plane[:, i * P : (i + 1) * P],
-                        rhs=w_words[:, l * CH_OUT + n0 : l * CH_OUT + n0 + BANK].bitcast(FP8X4),
-                        rhs_scale=w_planes[4 * l : P, n0 : n0 + BANK],
-                        start=True,
-                        stop=True,
-                    )
-                    if i % 2 == 0:
-                        nc.scalar.copy(out=planes[:, i, :], in_=acc[:])
-                    else:
-                        nc.vector.tensor_copy(out=planes[:, i, :], in_=acc[:])
-                for q in range(BANK // n_stage):
-                    stage = stage_pool.tile([P, STAGE_COLS], F32, tag="stage")
-                    nc.gpsimd.tensor_scalar(
-                        out=stage[:].rearrange("p (n i) -> p n i", i=d),
-                        in0=planes[:, :, q * n_stage : (q + 1) * n_stage].rearrange("p i n -> p n i"),
-                        scalar1=1.0,
-                        scalar2=0.0,
-                        op0=mybir.AluOpType.mult,
-                        op1=mybir.AluOpType.add,
-                    )
-                    c0 = out_start[l] + (n0 + q * n_stage) * d
-                    nc.sync.dma_start(out=out[bt * P : (bt + 1) * P, c0 : c0 + STAGE_COLS], in_=stage[:])
-
-        def multiply(bt, l):
-            if l == BY_PLANES:
-                multiply_by_planes(bt, l)
-            else:
-                multiply_unit(bt, l)
+                c0 = out_start[l] + n_first * d
+                nc.sync.dma_start(out=out[bt * P : (bt + 1) * P, c0 : c0 + n_group * d], in_=stage[:])
 
         n_units = len(units)
         for j in range(LOOKAHEAD + 1):
@@ -239,4 +202,4 @@ def tile_so3_linear_pa_t_kernel(
                 sort_unit(*units[j + LOOKAHEAD + 1])
             if j + LOOKAHEAD < n_units:
                 quantise_unit(*units[j + LOOKAHEAD])
-            multiply(*units[j])
+            multiply_unit(*units[j])

@@ -79,20 +79,17 @@ def tile_so3_linear_pa_t_kernel(
                 in_=w_words_in[l].rearrange("g p n t -> (g p) (n t)").bitcast(I32),
             )
 
-        load_x(0, 0)
-        load_x(0, 1)
-        for l in range(4):
+        def load_w_scales(l):
             rows = w_scales_in[l].rearrange("g (q r) n -> r (g q) n", r=4)
             for r in range(4):
                 nc.sync.dma_start(
                     out=w_planes[4 * l + r : P : 32, 0:CH_OUT].bitcast(I32), in_=rows[r].bitcast(I32)
                 )
-        load_w_words(0)
-        load_w_words(1)
-        load_x(0, 2)
-        load_w_words(2)
-        load_x(0, 3)
-        load_w_words(3)
+
+        for l in range(4):
+            load_x(0, l)
+            load_w_words(l)
+            load_w_scales(l)
         for bt in range(1, BATCH_TILES):
             for l in range(4):
                 load_x(bt, l)

@@ -48,8 +48,7 @@ def tile_so3_linear_pa_t_kernel(
         group_pool = ctx.enter_context(tc.tile_pool(name="group_pool", bufs=2))
         code_pool = ctx.enter_context(tc.tile_pool(name="code_pool", bufs=LOOKAHEAD + 2))
         stage_pool = ctx.enter_context(tc.tile_pool(name="stage_pool", bufs=12))
-        xt_pool = ctx.enter_context(tc.psum_pool(name="xt_pool", bufs=4))
-        acc_pool = ctx.enter_context(tc.psum_pool(name="acc_pool", bufs=4))
+        bank_pool = ctx.enter_context(tc.psum_pool(name="bank_pool", bufs=8))
 
         w_planes = const.tile([P, CH_OUT + SPILL], U8, align_bytes=64)
         nc.vector.memset(w_planes[:].bitcast(I32), 0)
@@ -86,8 +85,10 @@ def tile_so3_linear_pa_t_kernel(
                     out=w_planes[4 * l + r : P : 32, 0:CH_OUT].bitcast(I32), in_=rows[r].bitcast(I32)
                 )
 
+        load_x(0, 0)
         for l in range(4):
-            load_x(0, l)
+            if l + 1 < 4:
+                load_x(0, l + 1)
             load_w_words(l)
             load_w_scales(l)
         for bt in range(1, BATCH_TILES):
@@ -100,7 +101,7 @@ def tile_so3_linear_pa_t_kernel(
         bias_f32 = const.tile([P, CH_OUT], F32)
         for h in range(CH_OUT // BANK):
             cols = slice(h * BANK, (h + 1) * BANK)
-            bias_acc = acc_pool.tile([P, BANK], F32, tag="acc")
+            bias_acc = bank_pool.tile([P, BANK], F32, tag="bank")
             nc.tensor.matmul(out=bias_acc[:], lhsT=ones[:], rhs=bias_rows[:, cols], start=True, stop=True)
             nc.vector.tensor_copy(out=bias_f32[:, cols], in_=bias_acc[:])
 
@@ -129,7 +130,7 @@ def tile_so3_linear_pa_t_kernel(
             pairs = [(i0, min(i0 + 2, d)) for i0 in range(0, d, 2)]
             banks = []
             for i0, i1 in pairs:
-                xt = xt_pool.tile([P, 4, P], F32, tag="xt")
+                xt = bank_pool.tile([P, 4, P], F32, tag="bank")
                 for s in range(2 * (i1 - i0)):
                     w0 = (2 * i0 + s) * P
                     nc.tensor.transpose(out=xt[:, s, :], in_=xs_words[:, w0 : w0 + P], identity=ident[:])
@@ -163,7 +164,7 @@ def tile_so3_linear_pa_t_kernel(
                         rhs_scale = w_planes[4 * l : P, n0 : n0 + width]
                     else:
                         rhs_scale = w_planes_moved[4 * l : P, MOVED + n0 : MOVED + n0 + width]
-                    acc = acc_pool.tile([P, BANK], F32, tag="acc")
+                    acc = bank_pool.tile([P, BANK], F32, tag="bank")
                     for i in range(d):
                         nc.tensor.matmul_mx(
                             out=acc[:, i * kept : i * kept + width],

@@ -50,8 +50,11 @@ def tile_so3_linear_pa_t_kernel(
         stage_pool = ctx.enter_context(tc.tile_pool(name="stage_pool", bufs=12))
         bank_pool = ctx.enter_context(tc.psum_pool(name="bank_pool", bufs=8))
 
-        w_planes = const.tile([P, CH_OUT + SPILL], U8, align_bytes=64)
-        nc.vector.memset(w_planes[:].bitcast(I32), 0)
+        w_planes = []
+        for l in range(4):
+            w_plane = const.tile([P, CH_OUT + SPILL], U8, tag="w_plane%d" % l, align_bytes=64)
+            nc.vector.memset(w_plane[:].bitcast(I32), 0)
+            w_planes.append(w_plane)
         w_words = const.tile([P, 4 * CH_OUT + SPILL], U32, align_bytes=64)
         nc.vector.memset(w_words[:, 4 * CH_OUT :].bitcast(I32), 0)
         bias_rows = const.tile([P, CH_OUT], BF16)
@@ -82,7 +85,7 @@ def tile_so3_linear_pa_t_kernel(
             rows = w_scales_in[l].rearrange("g (q r) n -> r (g q) n", r=4)
             for r in range(4):
                 nc.sync.dma_start(
-                    out=w_planes[4 * l + r : P : 32, 0:CH_OUT].bitcast(I32), in_=rows[r].bitcast(I32)
+                    out=w_planes[l][r : P : 32, 0:CH_OUT].bitcast(I32), in_=rows[r].bitcast(I32)
                 )
 
         load_x(0, 0)
@@ -96,7 +99,7 @@ def tile_so3_linear_pa_t_kernel(
                 load_x(bt, l)
 
         w_planes_moved = const.tile([P, MOVED + CH_OUT + SPILL], U8, align_bytes=64)
-        nc.vector.tensor_copy(out=w_planes_moved[:, MOVED:].bitcast(I32), in_=w_planes[:].bitcast(I32))
+        nc.vector.tensor_copy(out=w_planes_moved[:, MOVED:].bitcast(I32), in_=w_planes[2][:].bitcast(I32))
 
         bias_f32 = const.tile([P, CH_OUT], F32)
         for h in range(CH_OUT // BANK):
@@ -161,9 +164,9 @@ def tile_so3_linear_pa_t_kernel(
                 stage = stage_pool.tile([P, n_group * d], F32, tag="stage")
                 for k, (n0, n_here) in enumerate(group):
                     if n0 % WINDOW == 0:
-                        rhs_scale = w_planes[4 * l : P, n0 : n0 + width]
+                        rhs_scale = w_planes[l][:, n0 : n0 + width]
                     else:
-                        rhs_scale = w_planes_moved[4 * l : P, MOVED + n0 : MOVED + n0 + width]
+                        rhs_scale = w_planes_moved[:, MOVED + n0 : MOVED + n0 + width]
                     acc = bank_pool.tile([P, BANK], F32, tag="bank")
                     for i in range(d):
                         nc.tensor.matmul_mx(

@@ -27,8 +27,7 @@ WINDOW = 64
 MOVED = 32
 
 BANKS_PER_STORE = 4
-SORT_RUNS = 4
-LOOKAHEAD = 2
+COPY_LAG = 2
 
 
 def tile_so3_linear_pa_t_kernel(
@@ -39,31 +38,32 @@ def tile_so3_linear_pa_t_kernel(
     w_scales_in = (W0_scales, W1_scales, W2_scales, W3_scales)
     x_start = [CH_IN * sum(IR_DIMS[:l]) for l in range(4)]
     out_start = [CH_OUT * sum(IR_DIMS[:l]) for l in range(4)]
-    units = [(bt, l) for bt in range(BATCH_TILES) for l in range(4)]
 
     with ExitStack() as ctx:
         const = ctx.enter_context(tc.tile_pool(name="const", bufs=1))
         x_pool = ctx.enter_context(tc.tile_pool(name="x_pool", bufs=BATCH_TILES))
-        sort_pool = ctx.enter_context(tc.tile_pool(name="sort_pool", bufs=3))
-        group_pool = ctx.enter_context(tc.tile_pool(name="group_pool", bufs=2))
-        code_pool = ctx.enter_context(tc.tile_pool(name="code_pool", bufs=LOOKAHEAD + 2))
+        sort_pool = ctx.enter_context(tc.tile_pool(name="sort_pool", bufs=1))
+        group_pool = ctx.enter_context(tc.tile_pool(name="group_pool", bufs=1))
+        code_pool = ctx.enter_context(tc.tile_pool(name="code_pool", bufs=2))
         stage_pool = ctx.enter_context(tc.tile_pool(name="stage_pool", bufs=12))
         bank_pool = ctx.enter_context(tc.psum_pool(name="bank_pool", bufs=8))
+        ctx.enter_context(tc.manual_schedule())
 
+        ident = const.tile([P, P], F32)
+        make_identity(nc, ident[:])
         w_planes = []
         for l in range(4):
             w_plane = const.tile([P, CH_OUT + SPILL], U8, tag="w_plane%d" % l, align_bytes=64)
-            nc.vector.memset(w_plane[:].bitcast(I32), 0)
             w_planes.append(w_plane)
-        w_words = const.tile([P, 4 * CH_OUT + SPILL], U32, align_bytes=64)
-        nc.vector.memset(w_words[:, 4 * CH_OUT :].bitcast(I32), 0)
         bias_rows = const.tile([P, CH_OUT], BF16)
-        nc.vector.memset(bias_rows[:], 0.0)
+        nc.vector.memset(bias_rows[:].bitcast(I32), 0)
+        nc.vector.memset(w_planes[0][:].bitcast(I32), 0)
+        for l in range(1, 4):
+            nc.gpsimd.memset(w_planes[l][:].bitcast(I32), 0)
+        w_words = const.tile([P, 4 * CH_OUT + SPILL], U32, align_bytes=64)
+        nc.gpsimd.memset(w_words[:, 4 * CH_OUT :].bitcast(I32), 0)
         ones = const.tile([P, P], BF16)
         nc.vector.memset(ones[:], 1.0)
-        ident = const.tile([P, P], F32)
-        make_identity(nc, ident[:])
-        nc.scalar.dma_start(out=bias_rows[0:1, :], in_=bias.unsqueeze(0))
 
         x_tiles = {}
 
@@ -84,123 +84,184 @@ def tile_so3_linear_pa_t_kernel(
         def load_w_scales(l):
             rows = w_scales_in[l].rearrange("g (q r) n -> r (g q) n", r=4)
             for r in range(4):
-                nc.sync.dma_start(
-                    out=w_planes[l][r : P : 32, 0:CH_OUT].bitcast(I32), in_=rows[r].bitcast(I32)
-                )
+                nc.sync.dma_start(out=w_planes[l][r : P : 32, 0:CH_OUT].bitcast(I32), in_=rows[r].bitcast(I32))
 
         load_x(0, 0)
+        nc.sync.dma_start(out=bias_rows[0:1, :], in_=bias.unsqueeze(0))
+        load_x(0, 1)
+        load_w_words(0)
+        load_w_scales(0)
+        load_x(0, 2)
+        load_w_words(1)
+        load_w_scales(1)
+        load_x(0, 3)
+        load_w_words(2)
+        load_w_scales(2)
+        load_w_words(3)
+        load_x(1, 0)
+        load_x(1, 1)
+        load_w_scales(3)
+        load_x(1, 2)
+        load_x(1, 3)
         for l in range(4):
-            if l + 1 < 4:
-                load_x(0, l + 1)
-            load_w_words(l)
-            load_w_scales(l)
-        for bt in range(1, BATCH_TILES):
-            for l in range(4):
-                load_x(bt, l)
+            load_x(2, l)
 
-        w_planes_moved = const.tile([P, MOVED + CH_OUT + SPILL], U8, align_bytes=64)
-        nc.vector.tensor_copy(out=w_planes_moved[:, MOVED:].bitcast(I32), in_=w_planes[2][:].bitcast(I32))
+        w_plane2_moved = const.tile([P, MOVED + CH_OUT + SPILL], U8, align_bytes=64)
+        nc.gpsimd.tensor_copy(out=w_plane2_moved[:, MOVED:].bitcast(I32), in_=w_planes[2][:].bitcast(I32))
 
         bias_f32 = const.tile([P, CH_OUT], F32)
-        for h in range(CH_OUT // BANK):
-            cols = slice(h * BANK, (h + 1) * BANK)
-            bias_acc = bank_pool.tile([P, BANK], F32, tag="bank")
-            nc.tensor.matmul(out=bias_acc[:], lhsT=ones[:], rhs=bias_rows[:, cols], start=True, stop=True)
-            nc.vector.tensor_copy(out=bias_f32[:, cols], in_=bias_acc[:])
 
         sorted_tiles = {}
+        turned_banks = {}
+        grouped_tiles = {}
         code_tiles = {}
+        pairs_of = [[(i0, min(i0 + 2, d)) for i0 in range(0, d, 2)] for d in IR_DIMS]
 
-        def sort_unit(bt, l):
+        def sort_part(bt, l, i0, i1):
             d = IR_DIMS[l]
-            x_seg = x_tiles[(bt, l)]
-            xs = sort_pool.tile([P, CH_IN * d], BF16, tag="xs")
-            src = x_seg[:].rearrange("b (p u e i) -> b u p e i", u=2, e=2, i=d)
-            dst = xs[:].rearrange("b (i u p e) -> b u p e i", u=2, p=P, e=2)
-            for i0 in range(0, d, SORT_RUNS):
-                i1 = min(i0 + SORT_RUNS, d)
-                for u in range(2):
-                    nc.vector.tensor_copy(out=dst[:, u, :, :, i0:i1], in_=src[:, u, :, :, i0:i1])
-            sorted_tiles[(bt, l)] = xs
+            if i0 == 0:
+                xs = sort_pool.tile([P, CH_IN * d], BF16, tag="xs%d" % l)
+                sorted_tiles[(bt, l)] = xs
+            src = x_tiles[(bt, l)][:].rearrange("b (p u e i) -> b u p e i", u=2, e=2, i=d)
+            dst = sorted_tiles[(bt, l)][:].rearrange("b (i u p e) -> b u p e i", u=2, p=P, e=2)
+            for u in range(2):
+                nc.vector.tensor_copy(out=dst[:, u, :, :, i0:i1], in_=src[:, u, :, :, i0:i1])
 
-        def quantise_unit(bt, l):
-            d = IR_DIMS[l]
+        def turn_pair(bt, l, i0, i1):
             xs_words = sorted_tiles[(bt, l)][:].bitcast(F32)
-            grouped = group_pool.tile([P, CH_IN * d], BF16, tag="grouped", align_bytes=64)
-            grouped_words = grouped[:].bitcast(F32)
-            codes = code_pool.tile([P, P * d], U32, tag="codes", align_bytes=64)
-            plane = code_pool.tile([P, P * d], U8, tag="plane", align_bytes=64)
-            pairs = [(i0, min(i0 + 2, d)) for i0 in range(0, d, 2)]
-            banks = []
-            for i0, i1 in pairs:
-                xt = bank_pool.tile([P, 4, P], F32, tag="bank")
-                for s in range(2 * (i1 - i0)):
-                    w0 = (2 * i0 + s) * P
-                    nc.tensor.transpose(out=xt[:, s, :], in_=xs_words[:, w0 : w0 + P], identity=ident[:])
-                banks.append(xt)
-            for (i0, i1), xt in zip(pairs, banks):
-                nc.scalar.copy(
-                    out=grouped_words[:, i0 * 2 * P : i1 * 2 * P].rearrange("p (i b u) -> p i b u", i=i1 - i0, u=2),
-                    in_=xt[:, 0 : 2 * (i1 - i0), :].rearrange("p (i u) b -> p i b u", u=2),
-                )
-            for i0, i1 in pairs:
-                nc.vector.quantize_mx(
-                    out=codes[:, i0 * P : i1 * P].bitcast(FP8X4),
-                    scales=plane[:, i0 * P : i1 * P],
-                    in_=grouped[:, i0 * 4 * P : i1 * 4 * P],
-                )
-            code_tiles[(bt, l)] = (codes, plane)
+            xt = bank_pool.tile([P, 4, P], F32, tag="bank")
+            for s in range(2 * (i1 - i0)):
+                w0 = (2 * i0 + s) * P
+                nc.tensor.transpose(out=xt[:, s, :], in_=xs_words[:, w0 : w0 + P], identity=ident[:])
+            turned_banks[(bt, l, i0)] = xt
 
-        def multiply_unit(bt, l):
-            d = IR_DIMS[l]
+        def group_pair(bt, l, i0, i1):
+            if i0 == 0:
+                grouped = group_pool.tile([P, CH_IN * IR_DIMS[l]], BF16, tag="grouped%d" % l, align_bytes=64)
+                grouped_tiles[(bt, l)] = grouped
+            grouped_words = grouped_tiles[(bt, l)][:].bitcast(F32)
+            nc.scalar.copy(
+                out=grouped_words[:, i0 * 2 * P : i1 * 2 * P].rearrange("p (i b u) -> p i b u", i=i1 - i0, u=2),
+                in_=turned_banks[(bt, l, i0)][:, 0 : 2 * (i1 - i0), :].rearrange("p (i u) b -> p i b u", u=2),
+            )
+
+        def quantise_pair(bt, l, i0, i1):
+            if i0 == 0:
+                codes = code_pool.tile([P, P * IR_DIMS[l]], U32, tag="codes%d" % l, align_bytes=64)
+                plane = code_pool.tile([P, P * IR_DIMS[l]], U8, tag="plane%d" % l, align_bytes=64)
+                code_tiles[(bt, l)] = (codes, plane)
+            codes, plane = code_tiles[(bt, l)]
+            nc.vector.quantize_mx(
+                out=codes[:, i0 * P : i1 * P].bitcast(FP8X4),
+                scales=plane[:, i0 * P : i1 * P],
+                in_=grouped_tiles[(bt, l)][:, i0 * 4 * P : i1 * 4 * P],
+            )
+
+        def each_pair(step, bt, l):
+            for i0, i1 in pairs_of[l]:
+                step(bt, l, i0, i1)
+
+        def spread_bias_multiply(h):
+            bias_acc = bank_pool.tile([P, BANK], F32, tag="bank")
+            nc.tensor.matmul(
+                out=bias_acc[:], lhsT=ones[:], rhs=bias_rows[:, h * BANK : (h + 1) * BANK], start=True, stop=True
+            )
+            return bias_acc
+
+        banks = []
+        for bt in range(BATCH_TILES):
+            for l in range(4):
+                kept = KEPT[l]
+                ranges = [(n0, min(kept, CH_OUT - n0)) for n0 in range(0, CH_OUT, kept)]
+                for first in range(0, len(ranges), BANKS_PER_STORE):
+                    group = ranges[first : first + BANKS_PER_STORE]
+                    n_group = sum(n_here for n0, n_here in group)
+                    for k, (n0, n_here) in enumerate(group):
+                        banks.append((bt, l, n0, n_here, group[0][0], n_group, first + k))
+        accs = {}
+        stages = {}
+
+        def multiply_bank(t):
+            bt, l, n0, n_here, n_first, n_group, k = banks[t]
             kept = KEPT[l]
             width = WIDTH[l]
             codes, plane = code_tiles[(bt, l)]
-            ranges = [(n0, min(kept, CH_OUT - n0)) for n0 in range(0, CH_OUT, kept)]
-            for first in range(0, len(ranges), BANKS_PER_STORE):
-                group = ranges[first : first + BANKS_PER_STORE]
-                n_first = group[0][0]
-                n_group = sum(n_here for n0, n_here in group)
+            if n0 % WINDOW == 0:
+                rhs_scale = w_planes[l][:, n0 : n0 + width]
+            else:
+                rhs_scale = w_plane2_moved[:, MOVED + n0 : MOVED + n0 + width]
+            acc = bank_pool.tile([P, BANK], F32, tag="bank")
+            for i in range(IR_DIMS[l]):
+                nc.tensor.matmul_mx(
+                    out=acc[:, i * kept : i * kept + width],
+                    lhsT=codes[:, i * P : (i + 1) * P].bitcast(FP8X4),
+                    lhsT_scale=plane[:, i * P : (i + 1) * P],
+                    rhs=w_words[:, l * CH_OUT + n0 : l * CH_OUT + n0 + width].bitcast(FP8X4),
+                    rhs_scale=rhs_scale,
+                    start=True,
+                    stop=True,
+                )
+            accs[t] = acc
+
+        def copy_bank(t):
+            bt, l, n0, n_here, n_first, n_group, k = banks[t]
+            d = IR_DIMS[l]
+            if n0 == n_first:
                 stage = stage_pool.tile([P, n_group * d], F32, tag="stage")
-                for k, (n0, n_here) in enumerate(group):
-                    if n0 % WINDOW == 0:
-                        rhs_scale = w_planes[l][:, n0 : n0 + width]
-                    else:
-                        rhs_scale = w_planes_moved[:, MOVED + n0 : MOVED + n0 + width]
-                    acc = bank_pool.tile([P, BANK], F32, tag="bank")
-                    for i in range(d):
-                        nc.tensor.matmul_mx(
-                            out=acc[:, i * kept : i * kept + width],
-                            lhsT=codes[:, i * P : (i + 1) * P].bitcast(FP8X4),
-                            lhsT_scale=plane[:, i * P : (i + 1) * P],
-                            rhs=w_words[:, l * CH_OUT + n0 : l * CH_OUT + n0 + width].bitcast(FP8X4),
-                            rhs_scale=rhs_scale,
-                            start=True,
-                            stop=True,
-                        )
-                    dst = stage[:, (n0 - n_first) * d : (n0 - n_first + n_here) * d]
-                    if l == 0:
-                        nc.vector.tensor_tensor(
-                            out=dst, in0=acc[:], in1=bias_f32[:, n0 : n0 + n_here], op=mybir.AluOpType.add
-                        )
-                    else:
-                        dst = dst.rearrange("p (n i) -> p n i", i=d)
-                        src = acc[:, 0 : d * kept].rearrange("p (i n) -> p n i", i=d)[:, 0:n_here, :]
-                        if (first + k) % 3 == 2:
-                            nc.vector.tensor_copy(out=dst, in_=src)
-                        else:
-                            nc.scalar.copy(out=dst, in_=src)
+                stages[(bt, l)] = stage
+            stage = stages[(bt, l)]
+            dst = stage[:, (n0 - n_first) * d : (n0 - n_first + n_here) * d]
+            if l == 0:
+                nc.vector.tensor_tensor(
+                    out=dst, in0=accs[t][:], in1=bias_f32[:, n0 : n0 + n_here], op=mybir.AluOpType.add
+                )
+            else:
+                dst = dst.rearrange("p (n i) -> p n i", i=d)
+                src = accs[t][:, 0 : d * KEPT[l]].rearrange("p (i n) -> p n i", i=d)[:, 0:n_here, :]
+                if k % 5 in (1, 3):
+                    nc.vector.tensor_copy(out=dst, in_=src)
+                else:
+                    nc.scalar.copy(out=dst, in_=src)
+            if n0 + n_here == n_first + n_group:
                 c0 = out_start[l] + n_first * d
                 nc.sync.dma_start(out=out[bt * P : (bt + 1) * P, c0 : c0 + n_group * d], in_=stage[:])
 
-        n_units = len(units)
-        for j in range(LOOKAHEAD + 1):
-            sort_unit(*units[j])
-        for j in range(LOOKAHEAD):
-            quantise_unit(*units[j])
-        for j in range(n_units):
-            if j + LOOKAHEAD + 1 < n_units:
-                sort_unit(*units[j + LOOKAHEAD + 1])
-            if j + LOOKAHEAD < n_units:
-                quantise_unit(*units[j + LOOKAHEAD])
-            multiply_unit(*units[j])
+        before = {}
+
+        def put(t, step, bt, l):
+            before.setdefault(t, []).append((step, bt, l))
+
+        n_banks = len(banks) // BATCH_TILES
+        put(0, sort_part, 0, 2)
+        put(2, turn_pair, 0, 2)
+        put(3, group_pair, 0, 2)
+        put(4, sort_part, 0, 3)
+        put(6, quantise_pair, 0, 2)
+        put(8, turn_pair, 0, 3)
+        put(9, group_pair, 0, 3)
+        put(12, quantise_pair, 0, 3)
+        for bt in range(1, BATCH_TILES):
+            for l, t in enumerate((14, 17, 21, 27)):
+                put((bt - 1) * n_banks + t, sort_part, bt, l)
+                put((bt - 1) * n_banks + t + 3, turn_pair, bt, l)
+                put((bt - 1) * n_banks + t + 4, group_pair, bt, l)
+                put((bt - 1) * n_banks + t + 6, quantise_pair, bt, l)
+
+        each_pair(sort_part, 0, 0)
+        each_pair(turn_pair, 0, 0)
+        each_pair(sort_part, 0, 1)
+        bias_accs = [spread_bias_multiply(h) for h in range(CH_OUT // BANK)]
+        each_pair(group_pair, 0, 0)
+        for h in range(CH_OUT // BANK):
+            nc.scalar.copy(out=bias_f32[:, h * BANK : (h + 1) * BANK], in_=bias_accs[h][:])
+        each_pair(turn_pair, 0, 1)
+        each_pair(quantise_pair, 0, 0)
+        each_pair(group_pair, 0, 1)
+        each_pair(quantise_pair, 0, 1)
+        for t in range(len(banks) + COPY_LAG):
+            for step, bt, l in before.get(t, []):
+                each_pair(step, bt, l)
+            if t < len(banks):
+                multiply_bank(t)
+            if t >= COPY_LAG:
+                copy_bank(t - COPY_LAG)

@@ -26,7 +26,7 @@ SPILL = 64
 WINDOW = 64
 MOVED = 32
 
-BANKS_PER_STORE = 4
+STORES = ((0, 4096), (4096, 9216), (9216, 12800), (12800, 16384))
 COPY_LAG = 2
 
 
@@ -41,11 +41,11 @@ def tile_so3_linear_pa_t_kernel(
 
     with ExitStack() as ctx:
         const = ctx.enter_context(tc.tile_pool(name="const", bufs=1))
-        x_pool = ctx.enter_context(tc.tile_pool(name="x_pool", bufs=BATCH_TILES))
+        x_pool = ctx.enter_context(tc.tile_pool(name="x_pool", bufs=2))
         sort_pool = ctx.enter_context(tc.tile_pool(name="sort_pool", bufs=1))
         group_pool = ctx.enter_context(tc.tile_pool(name="group_pool", bufs=1))
         code_pool = ctx.enter_context(tc.tile_pool(name="code_pool", bufs=2))
-        stage_pool = ctx.enter_context(tc.tile_pool(name="stage_pool", bufs=12))
+        stage_pool = ctx.enter_context(tc.tile_pool(name="stage_pool", bufs=2))
         bank_pool = ctx.enter_context(tc.psum_pool(name="bank_pool", bufs=8))
         ctx.enter_context(tc.manual_schedule())
 
@@ -172,17 +172,13 @@ def tile_so3_linear_pa_t_kernel(
         for bt in range(BATCH_TILES):
             for l in range(4):
                 kept = KEPT[l]
-                ranges = [(n0, min(kept, CH_OUT - n0)) for n0 in range(0, CH_OUT, kept)]
-                for first in range(0, len(ranges), BANKS_PER_STORE):
-                    group = ranges[first : first + BANKS_PER_STORE]
-                    n_group = sum(n_here for n0, n_here in group)
-                    for k, (n0, n_here) in enumerate(group):
-                        banks.append((bt, l, n0, n_here, group[0][0], n_group, first + k))
+                for n0 in range(0, CH_OUT, kept):
+                    banks.append((bt, l, n0, min(kept, CH_OUT - n0)))
         accs = {}
         stages = {}
 
         def multiply_bank(t):
-            bt, l, n0, n_here, n_first, n_group, k = banks[t]
+            bt, l, n0, n_here = banks[t]
             kept = KEPT[l]
             width = WIDTH[l]
             codes, plane = code_tiles[(bt, l)]
@@ -204,13 +200,17 @@ def tile_so3_linear_pa_t_kernel(
             accs[t] = acc
 
         def copy_bank(t):
-            bt, l, n0, n_here, n_first, n_group, k = banks[t]
+            bt, l, n0, n_here = banks[t]
             d = IR_DIMS[l]
-            if n0 == n_first:
-                stage = stage_pool.tile([P, n_group * d], F32, tag="stage")
-                stages[(bt, l)] = stage
-            stage = stages[(bt, l)]
-            dst = stage[:, (n0 - n_first) * d : (n0 - n_first + n_here) * d]
+            c0 = out_start[l] + n0 * d
+            c1 = c0 + n_here * d
+            store = [s for s in range(len(STORES)) if STORES[s][0] <= c0 < STORES[s][1]][0]
+            first, end = STORES[store]
+            if c0 == first:
+                stage = stage_pool.tile([P, end - first], F32, tag="stage%d" % min(store, 2))
+                stages[(bt, store)] = stage
+            stage = stages[(bt, store)]
+            dst = stage[:, c0 - first : c1 - first]
             if l == 0:
                 nc.vector.tensor_tensor(
                     out=dst, in0=accs[t][:], in1=bias_f32[:, n0 : n0 + n_here], op=mybir.AluOpType.add
@@ -218,13 +218,12 @@ def tile_so3_linear_pa_t_kernel(
             else:
                 dst = dst.rearrange("p (n i) -> p n i", i=d)
                 src = accs[t][:, 0 : d * KEPT[l]].rearrange("p (i n) -> p n i", i=d)[:, 0:n_here, :]
-                if k % 5 in (1, 3):
+                if (n0 // KEPT[l]) % 5 in (1, 3):
                     nc.vector.tensor_copy(out=dst, in_=src)
                 else:
                     nc.scalar.copy(out=dst, in_=src)
-            if n0 + n_here == n_first + n_group:
-                c0 = out_start[l] + n_first * d
-                nc.sync.dma_start(out=out[bt * P : (bt + 1) * P, c0 : c0 + n_group * d], in_=stage[:])
+            if c1 == end:
+                nc.sync.dma_start(out=out[bt * P : (bt + 1) * P, first:end], in_=stage[:])
 
         before = {}
 

@@ -26,7 +26,7 @@ SPILL = 64
 WINDOW = 64
 MOVED = 32
 
-STORES = ((0, 4096), (4096, 9216), (9216, 12800), (12800, 16384))
+STORES = ((0, 4096), (4096, 6496), (6496, 9216), (9216, 11904), (11904, 14144), (14144, 16384))
 COPY_LAG = 2
 
 
@@ -41,7 +41,7 @@ def tile_so3_linear_pa_t_kernel(
 
     with ExitStack() as ctx:
         const = ctx.enter_context(tc.tile_pool(name="const", bufs=1))
-        x_pool = ctx.enter_context(tc.tile_pool(name="x_pool", bufs=2))
+        x_pool = ctx.enter_context(tc.tile_pool(name="x_pool", bufs=BATCH_TILES))
         sort_pool = ctx.enter_context(tc.tile_pool(name="sort_pool", bufs=1))
         group_pool = ctx.enter_context(tc.tile_pool(name="group_pool", bufs=1))
         code_pool = ctx.enter_context(tc.tile_pool(name="code_pool", bufs=2))
@@ -65,15 +65,14 @@ def tile_so3_linear_pa_t_kernel(
         ones = const.tile([P, P], BF16)
         nc.vector.memset(ones[:], 1.0)
 
-        x_tiles = {}
+        x_tiles = []
 
-        def load_x(bt, l):
-            x_seg = x_pool.tile([P, CH_IN * IR_DIMS[l]], BF16, tag="x%d" % l)
-            nc.sync.dma_start(
-                out=x_seg[:],
-                in_=x[bt * P : (bt + 1) * P, x_start[l] : x_start[l] + CH_IN * IR_DIMS[l]],
-            )
-            x_tiles[(bt, l)] = x_seg
+        def load_x(bt, first_l, end_l):
+            if first_l == 0:
+                x_rows = x_pool.tile([P, CH_IN * sum(IR_DIMS)], BF16, tag="x_rows")
+                x_tiles.append(x_rows)
+            cols = slice(x_start[first_l], x_start[end_l - 1] + CH_IN * IR_DIMS[end_l - 1])
+            nc.sync.dma_start(out=x_tiles[bt][:, cols], in_=x[bt * P : (bt + 1) * P, cols])
 
         def load_w_words(l):
             nc.sync.dma_start(
@@ -86,25 +85,21 @@ def tile_so3_linear_pa_t_kernel(
             for r in range(4):
                 nc.sync.dma_start(out=w_planes[l][r : P : 32, 0:CH_OUT].bitcast(I32), in_=rows[r].bitcast(I32))
 
-        load_x(0, 0)
-        nc.sync.dma_start(out=bias_rows[0:1, :], in_=bias.unsqueeze(0))
-        load_x(0, 1)
+        load_x(0, 0, 1)
+        load_x(0, 1, 2)
         load_w_words(0)
+        nc.sync.dma_start(out=bias_rows[0:1, :], in_=bias.unsqueeze(0))
         load_w_scales(0)
-        load_x(0, 2)
+        load_x(0, 2, 3)
         load_w_words(1)
         load_w_scales(1)
-        load_x(0, 3)
+        load_x(0, 3, 4)
         load_w_words(2)
         load_w_scales(2)
         load_w_words(3)
-        load_x(1, 0)
-        load_x(1, 1)
+        load_x(1, 0, 4)
         load_w_scales(3)
-        load_x(1, 2)
-        load_x(1, 3)
-        for l in range(4):
-            load_x(2, l)
+        load_x(2, 0, 4)
 
         w_plane2_moved = const.tile([P, MOVED + CH_OUT + SPILL], U8, align_bytes=64)
         nc.gpsimd.tensor_copy(out=w_plane2_moved[:, MOVED:].bitcast(I32), in_=w_planes[2][:].bitcast(I32))
@@ -122,7 +117,8 @@ def tile_so3_linear_pa_t_kernel(
             if i0 == 0:
                 xs = sort_pool.tile([P, CH_IN * d], BF16, tag="xs%d" % l)
                 sorted_tiles[(bt, l)] = xs
-            src = x_tiles[(bt, l)][:].rearrange("b (p u e i) -> b u p e i", u=2, e=2, i=d)
+            x_seg = x_tiles[bt][:, x_start[l] : x_start[l] + CH_IN * d]
+            src = x_seg.rearrange("b (p u e i) -> b u p e i", u=2, e=2, i=d)
             dst = sorted_tiles[(bt, l)][:].rearrange("b (i u p e) -> b u p e i", u=2, p=P, e=2)
             for u in range(2):
                 nc.vector.tensor_copy(out=dst[:, u, :, :, i0:i1], in_=src[:, u, :, :, i0:i1])
@@ -207,7 +203,8 @@ def tile_so3_linear_pa_t_kernel(
             store = [s for s in range(len(STORES)) if STORES[s][0] <= c0 < STORES[s][1]][0]
             first, end = STORES[store]
             if c0 == first:
-                stage = stage_pool.tile([P, end - first], F32, tag="stage%d" % min(store, 2))
+                tag = "stage01" if store == 0 else "stage23"
+                stage = stage_pool.tile([P, end - first], F32, tag=tag, bufs=2 if store == 0 else 6)
                 stages[(bt, store)] = stage
             stage = stages[(bt, store)]
             dst = stage[:, c0 - first : c1 - first]
@@ -240,7 +237,7 @@ def tile_so3_linear_pa_t_kernel(
         put(9, group_pair, 0, 3)
         put(12, quantise_pair, 0, 3)
         for bt in range(1, BATCH_TILES):
-            for l, t in enumerate((14, 17, 21, 27)):
+            for l, t in enumerate((17, 19, 22, 27)):
                 put((bt - 1) * n_banks + t, sort_part, bt, l)
                 put((bt - 1) * n_banks + t + 3, turn_pair, bt, l)
                 put((bt - 1) * n_banks + t + 4, group_pair, bt, l)

@@ -26,7 +26,8 @@ SPILL = 64
 WINDOW = 64
 MOVED = 32
 
-STORES = ((0, 4096), (4096, 6496), (6496, 9216), (9216, 11904), (11904, 14144), (14144, 16384))
+STORES = ((0, 4096), (4096, 6976), (6976, 9216), (9216, 11904), (11904, 14144), (14144, 16384))
+DMA_ALIGN = 256
 COPY_LAG = 2
 
 
@@ -53,14 +54,14 @@ def tile_so3_linear_pa_t_kernel(
         make_identity(nc, ident[:])
         w_planes = []
         for l in range(4):
-            w_plane = const.tile([P, CH_OUT + SPILL], U8, tag="w_plane%d" % l, align_bytes=64)
+            w_plane = const.tile([P, CH_OUT + SPILL], U8, tag="w_plane%d" % l, align_bytes=DMA_ALIGN)
             w_planes.append(w_plane)
         bias_rows = const.tile([P, CH_OUT], BF16)
         nc.vector.memset(bias_rows[:].bitcast(I32), 0)
         nc.vector.memset(w_planes[0][:].bitcast(I32), 0)
         for l in range(1, 4):
             nc.gpsimd.memset(w_planes[l][:].bitcast(I32), 0)
-        w_words = const.tile([P, 4 * CH_OUT + SPILL], U32, align_bytes=64)
+        w_words = const.tile([P, 4 * CH_OUT + SPILL], U32, align_bytes=DMA_ALIGN)
         nc.gpsimd.memset(w_words[:, 4 * CH_OUT :].bitcast(I32), 0)
         ones = const.tile([P, P], BF16)
         nc.vector.memset(ones[:], 1.0)
@@ -69,7 +70,7 @@ def tile_so3_linear_pa_t_kernel(
 
         def load_x(bt, first_l, end_l):
             if first_l == 0:
-                x_rows = x_pool.tile([P, CH_IN * sum(IR_DIMS)], BF16, tag="x_rows")
+                x_rows = x_pool.tile([P, CH_IN * sum(IR_DIMS)], BF16, tag="x_rows", align_bytes=DMA_ALIGN)
                 x_tiles.append(x_rows)
             cols = slice(x_start[first_l], x_start[end_l - 1] + CH_IN * IR_DIMS[end_l - 1])
             nc.sync.dma_start(out=x_tiles[bt][:, cols], in_=x[bt * P : (bt + 1) * P, cols])
@@ -85,8 +86,7 @@ def tile_so3_linear_pa_t_kernel(
             for r in range(4):
                 nc.sync.dma_start(out=w_planes[l][r : P : 32, 0:CH_OUT].bitcast(I32), in_=rows[r].bitcast(I32))
 
-        load_x(0, 0, 1)
-        load_x(0, 1, 2)
+        load_x(0, 0, 2)
         load_w_words(0)
         nc.sync.dma_start(out=bias_rows[0:1, :], in_=bias.unsqueeze(0))
         load_w_scales(0)
@@ -204,7 +204,7 @@ def tile_so3_linear_pa_t_kernel(
             first, end = STORES[store]
             if c0 == first:
                 tag = "stage01" if store == 0 else "stage23"
-                stage = stage_pool.tile([P, end - first], F32, tag=tag, bufs=2 if store == 0 else 6)
+                stage = stage_pool.tile([P, end - first], F32, tag=tag, bufs=2 if store == 0 else 6, align_bytes=DMA_ALIGN)
                 stages[(bt, store)] = stage
             stage = stages[(bt, store)]
             dst = stage[:, c0 - first : c1 - first]

from contextlib import ExitStack

import concourse.mybir as mybir
from concourse.masks import make_identity

BF16 = mybir.dt.bfloat16
F32 = mybir.dt.float32
I32 = mybir.dt.int32
U32 = mybir.dt.uint32
U8 = mybir.dt.uint8
FP8X4 = mybir.dt.float8_e4m3fn_x4

P = 128
BATCH = 384
CH_IN = 512
CH_OUT = 1024
IR_DIMS = (1, 3, 5, 7)
BANK = 512
BATCH_TILES = BATCH // P

FLOPS = 2 * BATCH * sum(IR_DIMS) * CH_IN * CH_OUT

WIDTH = (512, 128, 128, 128)
KEPT = (512, 128, 96, 64)
SPILL = 64
WINDOW = 64
MOVED = 32

STORES = ((0, 4096), (4096, 6976), (6976, 9216), (9216, 11904), (11904, 14144), (14144, 16384))
DMA_ALIGN = 256
COPY_LAG = 2


def tile_so3_linear_pa_t_kernel(
    tc, x, W0_words, W0_scales, W1_words, W1_scales, W2_words, W2_scales, W3_words, W3_scales, bias, out
):
    nc = tc.nc
    w_words_in = (W0_words, W1_words, W2_words, W3_words)
    w_scales_in = (W0_scales, W1_scales, W2_scales, W3_scales)
    x_start = [CH_IN * sum(IR_DIMS[:l]) for l in range(4)]
    out_start = [CH_OUT * sum(IR_DIMS[:l]) for l in range(4)]

    with ExitStack() as ctx:
        const = ctx.enter_context(tc.tile_pool(name="const", bufs=1))
        x_pool = ctx.enter_context(tc.tile_pool(name="x_pool", bufs=BATCH_TILES))
        sort_pool = ctx.enter_context(tc.tile_pool(name="sort_pool", bufs=1))
        group_pool = ctx.enter_context(tc.tile_pool(name="group_pool", bufs=1))
        code_pool = ctx.enter_context(tc.tile_pool(name="code_pool", bufs=2))
        stage_pool = ctx.enter_context(tc.tile_pool(name="stage_pool", bufs=2))
        bank_pool = ctx.enter_context(tc.psum_pool(name="bank_pool", bufs=8))
        ctx.enter_context(tc.manual_schedule())

        ident = const.tile([P, P], F32)
        make_identity(nc, ident[:])
        w_planes = []
        for l in range(4):
            w_plane = const.tile([P, CH_OUT + SPILL], U8, tag="w_plane%d" % l, align_bytes=DMA_ALIGN)
            w_planes.append(w_plane)
        bias_rows = const.tile([P, CH_OUT], BF16)
        nc.vector.memset(bias_rows[:].bitcast(I32), 0)
        nc.vector.memset(w_planes[0][:].bitcast(I32), 0)
        for l in range(1, 4):
            nc.gpsimd.memset(w_planes[l][:].bitcast(I32), 0)
        w_words = const.tile([P, 4 * CH_OUT + SPILL], U32, align_bytes=DMA_ALIGN)
        nc.gpsimd.memset(w_words[:, 4 * CH_OUT :].bitcast(I32), 0)
        ones = const.tile([P, P], BF16)
        nc.vector.memset(ones[:], 1.0)

        x_tiles = []

        def load_x(bt, first_l, end_l):
            if first_l == 0:
                x_rows = x_pool.tile([P, CH_IN * sum(IR_DIMS)], BF16, tag="x_rows", align_bytes=DMA_ALIGN)
                x_tiles.append(x_rows)
            cols = slice(x_start[first_l], x_start[end_l - 1] + CH_IN * IR_DIMS[end_l - 1])
            nc.sync.dma_start(out=x_tiles[bt][:, cols], in_=x[bt * P : (bt + 1) * P, cols])

        def load_w_words(l):
            nc.sync.dma_start(
                out=w_words[:, l * CH_OUT : (l + 1) * CH_OUT].bitcast(I32),
                in_=w_words_in[l].rearrange("g p n t -> (g p) (n t)").bitcast(I32),
            )

        def load_w_scales(l):
            rows = w_scales_in[l].rearrange("g (q r) n -> r (g q) n", r=4)
            for r in range(4):
                nc.sync.dma_start(out=w_planes[l][r : P : 32, 0:CH_OUT].bitcast(I32), in_=rows[r].bitcast(I32))

        load_x(0, 0, 2)
        load_w_words(0)
        nc.sync.dma_start(out=bias_rows[0:1, :], in_=bias.unsqueeze(0))
        load_w_scales(0)
        load_x(0, 2, 3)
        load_w_words(1)
        load_w_scales(1)
        load_x(0, 3, 4)
        load_w_words(2)
        load_w_scales(2)
        load_w_words(3)
        load_x(1, 0, 4)
        load_w_scales(3)
        load_x(2, 0, 4)

        w_plane2_moved = const.tile([P, MOVED + CH_OUT + SPILL], U8, align_bytes=64)
        nc.gpsimd.tensor_copy(out=w_plane2_moved[:, MOVED:].bitcast(I32), in_=w_planes[2][:].bitcast(I32))

        bias_f32 = const.tile([P, CH_OUT], F32)

        sorted_tiles = {}
        turned_banks = {}
        grouped_tiles = {}
        code_tiles = {}
        pairs_of = [[(i0, min(i0 + 2, d)) for i0 in range(0, d, 2)] for d in IR_DIMS]

        def sort_part(bt, l, i0, i1):
            d = IR_DIMS[l]
            if i0 == 0:
                xs = sort_pool.tile([P, CH_IN * d], BF16, tag="xs%d" % l)
                sorted_tiles[(bt, l)] = xs
            x_seg = x_tiles[bt][:, x_start[l] : x_start[l] + CH_IN * d]
            src = x_seg.rearrange("b (p u e i) -> b u p e i", u=2, e=2, i=d)
            dst = sorted_tiles[(bt, l)][:].rearrange("b (i u p e) -> b u p e i", u=2, p=P, e=2)
            for u in range(2):
                nc.vector.tensor_copy(out=dst[:, u, :, :, i0:i1], in_=src[:, u, :, :, i0:i1])

        def turn_pair(bt, l, i0, i1):
            xs_words = sorted_tiles[(bt, l)][:].bitcast(F32)
            xt = bank_pool.tile([P, 4, P], F32, tag="bank")
            for s in range(2 * (i1 - i0)):
                w0 = (2 * i0 + s) * P
                nc.tensor.transpose(out=xt[:, s, :], in_=xs_words[:, w0 : w0 + P], identity=ident[:])
            turned_banks[(bt, l, i0)] = xt

        def group_pair(bt, l, i0, i1):
            if i0 == 0:
                grouped = group_pool.tile([P, CH_IN * IR_DIMS[l]], BF16, tag="grouped%d" % l, align_bytes=64)
                grouped_tiles[(bt, l)] = grouped
            grouped_words = grouped_tiles[(bt, l)][:].bitcast(F32)
            nc.scalar.copy(
                out=grouped_words[:, i0 * 2 * P : i1 * 2 * P].rearrange("p (i b u) -> p i b u", i=i1 - i0, u=2),
                in_=turned_banks[(bt, l, i0)][:, 0 : 2 * (i1 - i0), :].rearrange("p (i u) b -> p i b u", u=2),
            )

        def quantise_pair(bt, l, i0, i1):
            if i0 == 0:
                codes = code_pool.tile([P, P * IR_DIMS[l]], U32, tag="codes%d" % l, align_bytes=64)
                plane = code_pool.tile([P, P * IR_DIMS[l]], U8, tag="plane%d" % l, align_bytes=64)
                code_tiles[(bt, l)] = (codes, plane)
            codes, plane = code_tiles[(bt, l)]
            nc.vector.quantize_mx(
                out=codes[:, i0 * P : i1 * P].bitcast(FP8X4),
                scales=plane[:, i0 * P : i1 * P],
                in_=grouped_tiles[(bt, l)][:, i0 * 4 * P : i1 * 4 * P],
            )

        def each_pair(step, bt, l):
            for i0, i1 in pairs_of[l]:
                step(bt, l, i0, i1)

        def spread_bias_multiply(h):
            bias_acc = bank_pool.tile([P, BANK], F32, tag="bank")
            nc.tensor.matmul(
                out=bias_acc[:], lhsT=ones[:], rhs=bias_rows[:, h * BANK : (h + 1) * BANK], start=True, stop=True
            )
            return bias_acc

        banks = []
        for bt in range(BATCH_TILES):
            for l in range(4):
                kept = KEPT[l]
                for n0 in range(0, CH_OUT, kept):
                    banks.append((bt, l, n0, min(kept, CH_OUT - n0)))
        accs = {}
        stages = {}

        def multiply_bank(t):
            bt, l, n0, n_here = banks[t]
            kept = KEPT[l]
            width = WIDTH[l]
            codes, plane = code_tiles[(bt, l)]
            if n0 % WINDOW == 0:
                rhs_scale = w_planes[l][:, n0 : n0 + width]
            else:
                rhs_scale = w_plane2_moved[:, MOVED + n0 : MOVED + n0 + width]
            acc = bank_pool.tile([P, BANK], F32, tag="bank")
            for i in range(IR_DIMS[l]):
                nc.tensor.matmul_mx(
                    out=acc[:, i * kept : i * kept + width],
                    lhsT=codes[:, i * P : (i + 1) * P].bitcast(FP8X4),
                    lhsT_scale=plane[:, i * P : (i + 1) * P],
                    rhs=w_words[:, l * CH_OUT + n0 : l * CH_OUT + n0 + width].bitcast(FP8X4),
                    rhs_scale=rhs_scale,
                    start=True,
                    stop=True,
                )
            accs[t] = acc

        def copy_bank(t):
            bt, l, n0, n_here = banks[t]
            d = IR_DIMS[l]
            c0 = out_start[l] + n0 * d
            c1 = c0 + n_here * d
            store = [s for s in range(len(STORES)) if STORES[s][0] <= c0 < STORES[s][1]][0]
            first, end = STORES[store]
            if c0 == first:
                tag = "stage01" if store == 0 else "stage23"
                stage = stage_pool.tile([P, end - first], F32, tag=tag, bufs=2 if store == 0 else 6, align_bytes=DMA_ALIGN)
                stages[(bt, store)] = stage
            stage = stages[(bt, store)]
            dst = stage[:, c0 - first : c1 - first]
            if l == 0:
                nc.vector.tensor_tensor(
                    out=dst, in0=accs[t][:], in1=bias_f32[:, n0 : n0 + n_here], op=mybir.AluOpType.add
                )
            else:
                dst = dst.rearrange("p (n i) -> p n i", i=d)
                src = accs[t][:, 0 : d * KEPT[l]].rearrange("p (i n) -> p n i", i=d)[:, 0:n_here, :]
                if (n0 // KEPT[l]) % 5 in (1, 3):
                    nc.vector.tensor_copy(out=dst, in_=src)
                else:
                    nc.scalar.copy(out=dst, in_=src)
            if c1 == end:
                nc.sync.dma_start(out=out[bt * P : (bt + 1) * P, first:end], in_=stage[:])

        before = {}

        def put(t, step, bt, l):
            before.setdefault(t, []).append((step, bt, l))

        n_banks = len(banks) // BATCH_TILES
        put(0, sort_part, 0, 2)
        put(2, turn_pair, 0, 2)
        put(3, group_pair, 0, 2)
        put(4, sort_part, 0, 3)
        put(6, quantise_pair, 0, 2)
        put(8, turn_pair, 0, 3)
        put(9, group_pair, 0, 3)
        put(12, quantise_pair, 0, 3)
        for bt in range(1, BATCH_TILES):
            for l, t in enumerate((17, 19, 22, 27)):
                put((bt - 1) * n_banks + t, sort_part, bt, l)
                put((bt - 1) * n_banks + t + 3, turn_pair, bt, l)
                put((bt - 1) * n_banks + t + 4, group_pair, bt, l)
                put((bt - 1) * n_banks + t + 6, quantise_pair, bt, l)

        each_pair(sort_part, 0, 0)
        each_pair(turn_pair, 0, 0)
        each_pair(sort_part, 0, 1)
        bias_accs = [spread_bias_multiply(h) for h in range(CH_OUT // BANK)]
        each_pair(group_pair, 0, 0)
        for h in range(CH_OUT // BANK):
            nc.scalar.copy(out=bias_f32[:, h * BANK : (h + 1) * BANK], in_=bias_accs[h][:])
        each_pair(turn_pair, 0, 1)
        each_pair(quantise_pair, 0, 0)
        each_pair(group_pair, 0, 1)
        each_pair(quantise_pair, 0, 1)
        for t in range(len(banks) + COPY_LAG):
            for step, bt, l in before.get(t, []):
                each_pair(step, bt, l)
            if t < len(banks):
                multiply_bank(t)
            if t >= COPY_LAG:
                copy_bank(t - COPY_LAG)
